import numpy as np
import ml_dtypes


def mxq(x, axis, fmt="e4m3"):
    dtype, down = {"e4m3": (ml_dtypes.float8_e4m3fn, 7), "e5m2": (ml_dtypes.float8_e5m2, 14)}[fmt]
    v = np.moveaxis(np.asarray(x, np.float32).astype(ml_dtypes.bfloat16).astype(np.float64), axis, -1)
    blocks = v.reshape(v.shape[:-1] + (-1, 32))
    amax = np.abs(blocks).max(-1, keepdims=True)
    byte = np.maximum(np.where(amax > 0, np.frexp(amax)[1] - 1 + 127, 0) - down, 1)
    scale = np.exp2(byte - 127.0)
    codes = (blocks / scale).astype(np.float32).astype(dtype).astype(np.float64)
    return np.moveaxis((codes * scale).reshape(v.shape), -1, axis)


WIDE = False


def mx_kscale(k):
    if not WIDE:
        return np.ones(k)
    levels = np.array([20, -20, 10, -10, 0])
    a = np.random.permutation(np.resize(levels, k // 512 * 4)).reshape(k // 512, 4)
    idx = np.arange(k)
    return np.exp2(a[idx // 512, idx % 128 // 32])


BF16 = ml_dtypes.bfloat16


def bf(x):
    return np.asarray(x, np.float32).astype(BF16)


def f64(x):
    return np.asarray(x).astype(np.float64)


B, Nb1, Nw1, Nb2x, Nb2y, Nw2x, Nw2y, R, C = 512, 2, 8, 4, 2, 16, 16, 64, 2
J1 = Nb1 * Nb1
K1 = C * Nw1 * Nw1
J3 = Nb2x * Nb2y
L1 = J3 * R
J2 = J3 * J1


def setup_inputs():
    s = mx_kscale(B)
    x = np.random.standard_normal((B, Nb1, Nw1, Nb1, Nw1, C)) * s[:, None, None, None, None, None]
    k1 = np.random.standard_normal((J1, K1, L1)) / np.sqrt(K1)
    b1 = np.random.standard_normal((1, J1, L1)) * 0.3
    g = np.random.standard_normal((B, J2, R)) * np.exp2(np.random.randint(-12, 1, (B, 1, 1))) / s[:, None, None]
    return {"x": bf(x.reshape(B, Nb1 * Nw1 * Nb1 * Nw1, C)),
            "k1": bf(k1),
            "b1": bf(b1),
            "grad_out": bf(g)}


def reference(x, k1, b1, grad_out):
    h = f64(x).reshape(B, Nb1, Nw1, Nb1, Nw1, C).transpose(0, 1, 3, 2, 4, 5).reshape(B, J1, K1)
    gy = f64(grad_out).reshape(B, R, J1, J3).transpose(0, 2, 3, 1).reshape(B, J1, L1)
    hq = mxq(h, 0, "e4m3").transpose(1, 2, 0)
    gq = mxq(gy, 0, "e5m2").transpose(1, 0, 2)
    return hq @ gq

@@ -1,0 +1,108 @@
+import concourse.mybir as mybir
+
+BF16 = mybir.dt.bfloat16
+F32 = mybir.dt.float32
+U32 = mybir.dt.uint32
+U8 = mybir.dt.uint8
+E4M3_X4 = mybir.dt.float8_e4m3fn_x4
+E5M2_X4 = mybir.dt.float8_e5m2_x4
+
+P = 128
+PACK = 4
+SAMPLES = P * PACK
+
+BLOCKS = 4
+BLOCK_SIDE = 2
+WINDOW_ROWS = 8
+HALVES = 2
+RUN = 8
+K1 = WINDOW_ROWS * HALVES * RUN
+
+R = 64
+M = 8
+L1 = R * M
+
+G_CHUNKS = 4
+R_CHUNK = R // G_CHUNKS
+
+FLOPS = 2 * BLOCKS * K1 * L1 * SAMPLES
+BYTES = 2 * SAMPLES * BLOCKS * K1 + 2 * SAMPLES * BLOCKS * L1 + 4 * BLOCKS * K1 * L1
+
+
+def tile_switchnet_fstar_pa_s_kernel(tc, x, k1, b1, grad_out, out):
+    nc = tc.nc
+
+    def regroup(j, dst, src):
+        if j < BLOCKS // 2:
+            nc.vector.tensor_copy(out=dst, in_=src)
+        else:
+            nc.scalar.copy(out=dst, in_=src)
+
+    with tc.tile_pool(name="keep", bufs=1) as keep, tc.psum_pool(name="psum", bufs=BLOCKS) as psum:
+        x_raw = keep.tile([P, PACK, BLOCK_SIDE, WINDOW_ROWS, BLOCK_SIDE, HALVES, RUN], BF16)
+        nc.sync.dma_start(
+            out=x_raw[:].rearrange("p t a w b h i -> p t (a w b h i)"),
+            in_=x.rearrange("(p t) g c -> p t (g c)", t=PACK),
+        )
+        g_rows = grad_out.rearrange("(p t) a c -> p t (a c)", t=PACK)
+        g_raw = []
+        for c in range(G_CHUNKS):
+            chunk = keep.tile([P, PACK, R_CHUNK, BLOCKS, M], BF16, name="g_raw%d" % c)
+            width = R_CHUNK * BLOCKS * M
+            nc.sync.dma_start(
+                out=chunk[:].rearrange("p t r j m -> p t (r j m)"),
+                in_=g_rows[:, :, c * width : (c + 1) * width],
+            )
+            g_raw.append(chunk)
+
+        x_grouped = keep.tile([P, BLOCKS, WINDOW_ROWS, HALVES, RUN, PACK], BF16, align_bytes=64)
+        x_codes = keep.tile([P, BLOCKS, K1], U32, align_bytes=64)
+        x_scales = keep.tile([P, BLOCKS, K1], U8, align_bytes=64)
+        for j in range(BLOCKS):
+            for h in range(HALVES):
+                regroup(
+                    j,
+                    x_grouped[:, j, :, h, :, :].rearrange("p w i t -> p w t i"),
+                    x_raw[:, :, j // BLOCK_SIDE, :, j % BLOCK_SIDE, h, :].rearrange("p t w i -> p w t i"),
+                )
+        nc.vector.quantize_mx(
+            out=x_codes[:].rearrange("p j k -> p (j k)").bitcast(E4M3_X4),
+            scales=x_scales[:].rearrange("p j k -> p (j k)"),
+            in_=x_grouped[:].rearrange("p j w h i t -> p (j w h i t)"),
+        )
+
+        g_grouped = keep.tile([P, BLOCKS, R, M, PACK], BF16, align_bytes=64)
+        g_codes = keep.tile([P, BLOCKS, R, M], U32, align_bytes=64)
+        g_scales = keep.tile([P, BLOCKS, R, M], U8, align_bytes=64)
+        for c in range(G_CHUNKS):
+            r_range = slice(c * R_CHUNK, (c + 1) * R_CHUNK)
+            for j in range(BLOCKS):
+                regroup(
+                    j,
+                    g_grouped[:, j, r_range, :, :].rearrange("p r m t -> p r t m"),
+                    g_raw[c][:, :, :, j, :].rearrange("p t r m -> p r t m"),
+                )
+            for j in range(BLOCKS):
+                nc.vector.quantize_mx(
+                    out=g_codes[:, j, r_range, :].rearrange("p r m -> p (r m)").bitcast(E5M2_X4),
+                    scales=g_scales[:, j, r_range, :].rearrange("p r m -> p (r m)"),
+                    in_=g_grouped[:, j, r_range, :, :].rearrange("p r m t -> p (r m t)"),
+                )
+
+        for j in range(BLOCKS):
+            acc = psum.tile([P, R, M], F32)
+            nc.tensor.matmul_mx(
+                out=acc[:].rearrange("p r m -> p (r m)"),
+                lhsT=x_codes[:, j, :].bitcast(E4M3_X4),
+                lhsT_scale=x_scales[:, j, :],
+                rhs=g_codes[:, j, :, :].rearrange("p r m -> p (r m)").bitcast(E5M2_X4),
+                rhs_scale=g_scales[:, j, :, :].rearrange("p r m -> p (r m)"),
+                start=True,
+                stop=True,
+            )
+            result = keep.tile([P, M, R], F32, name="result%d" % j)
+            if j % 2 == 0:
+                nc.scalar.copy(out=result[:], in_=acc[:].rearrange("p r m -> p m r"))
+            else:
+                nc.vector.tensor_copy(out=result[:], in_=acc[:].rearrange("p r m -> p m r"))
+            nc.sync.dma_start(out=out[j], in_=result[:].rearrange("p m r -> p (m r)"))

@@ -22,8 +22,8 @@ R = 64
 M = 8
 L1 = R * M
 
-G_CHUNKS = 4
-R_CHUNK = R // G_CHUNKS
+R_CHUNKS = (16, 16, 32)
+assert sum(R_CHUNKS) == R
 
 FLOPS = 2 * BLOCKS * K1 * L1 * SAMPLES
 BYTES = 2 * SAMPLES * BLOCKS * K1 + 2 * SAMPLES * BLOCKS * L1 + 4 * BLOCKS * K1 * L1
@@ -32,13 +32,7 @@ BYTES = 2 * SAMPLES * BLOCKS * K1 + 2 * SAMPLES * BLOCKS * L1 + 4 * BLOCKS * K1 
 def tile_switchnet_fstar_pa_s_kernel(tc, x, k1, b1, grad_out, out):
     nc = tc.nc
 
-    def regroup(j, dst, src):
-        if j < BLOCKS // 2:
-            nc.vector.tensor_copy(out=dst, in_=src)
-        else:
-            nc.scalar.copy(out=dst, in_=src)
-
-    with tc.tile_pool(name="keep", bufs=1) as keep, tc.psum_pool(name="psum", bufs=BLOCKS) as psum:
+    with tc.tile_pool(name="keep", bufs=1) as keep, tc.psum_pool(name="psum", bufs=BLOCKS) as psum, tc.manual_schedule():
         x_raw = keep.tile([P, PACK, BLOCK_SIDE, WINDOW_ROWS, BLOCK_SIDE, HALVES, RUN], BF16)
         nc.sync.dma_start(
             out=x_raw[:].rearrange("p t a w b h i -> p t (a w b h i)"),
@@ -46,48 +40,65 @@ def tile_switchnet_fstar_pa_s_kernel(tc, x, k1, b1, grad_out, out):
         )
         g_rows = grad_out.rearrange("(p t) a c -> p t (a c)", t=PACK)
         g_raw = []
-        for c in range(G_CHUNKS):
-            chunk = keep.tile([P, PACK, R_CHUNK, BLOCKS, M], BF16, name="g_raw%d" % c)
-            width = R_CHUNK * BLOCKS * M
+        r_first = []
+        for c, r_count in enumerate(R_CHUNKS):
+            r_first.append(sum(R_CHUNKS[:c]))
+            chunk = keep.tile([P, PACK, r_count, BLOCKS, M], BF16, name="g_raw%d" % c)
             nc.sync.dma_start(
                 out=chunk[:].rearrange("p t r j m -> p t (r j m)"),
-                in_=g_rows[:, :, c * width : (c + 1) * width],
+                in_=g_rows[:, :, r_first[c] * BLOCKS * M : (r_first[c] + r_count) * BLOCKS * M],
             )
             g_raw.append(chunk)
 
         x_grouped = keep.tile([P, BLOCKS, WINDOW_ROWS, HALVES, RUN, PACK], BF16, align_bytes=64)
         x_codes = keep.tile([P, BLOCKS, K1], U32, align_bytes=64)
         x_scales = keep.tile([P, BLOCKS, K1], U8, align_bytes=64)
-        for j in range(BLOCKS):
-            for h in range(HALVES):
-                regroup(
-                    j,
-                    x_grouped[:, j, :, h, :, :].rearrange("p w i t -> p w t i"),
-                    x_raw[:, :, j // BLOCK_SIDE, :, j % BLOCK_SIDE, h, :].rearrange("p t w i -> p w t i"),
-                )
-        nc.vector.quantize_mx(
-            out=x_codes[:].rearrange("p j k -> p (j k)").bitcast(E4M3_X4),
-            scales=x_scales[:].rearrange("p j k -> p (j k)"),
-            in_=x_grouped[:].rearrange("p j w h i t -> p (j w h i t)"),
-        )
-
         g_grouped = keep.tile([P, BLOCKS, R, M, PACK], BF16, align_bytes=64)
         g_codes = keep.tile([P, BLOCKS, R, M], U32, align_bytes=64)
         g_scales = keep.tile([P, BLOCKS, R, M], U8, align_bytes=64)
-        for c in range(G_CHUNKS):
-            r_range = slice(c * R_CHUNK, (c + 1) * R_CHUNK)
-            for j in range(BLOCKS):
-                regroup(
-                    j,
-                    g_grouped[:, j, r_range, :, :].rearrange("p r m t -> p r t m"),
-                    g_raw[c][:, :, :, j, :].rearrange("p t r m -> p r t m"),
+
+        pieces = []
+        for j in range(BLOCKS):
+            copies = [
+                (
+                    x_grouped[:, j, :, h, :, :].rearrange("p w i t -> p w t i"),
+                    x_raw[:, :, j // BLOCK_SIDE, :, j % BLOCK_SIDE, h, :].rearrange("p t w i -> p w t i"),
                 )
+                for h in range(HALVES)
+            ]
+            quantise = dict(
+                out=x_codes[:, j, :].bitcast(E4M3_X4),
+                scales=x_scales[:, j, :],
+                in_=x_grouped[:, j].rearrange("p w h i t -> p (w h i t)"),
+            )
+            pieces.append((copies, quantise))
+        for c, r_count in enumerate(R_CHUNKS):
+            r_range = slice(r_first[c], r_first[c] + r_count)
             for j in range(BLOCKS):
-                nc.vector.quantize_mx(
+                copies = [
+                    (
+                        g_grouped[:, j, r_first[c] + lo : r_first[c] + lo + r_count // 2, :, :].rearrange(
+                            "p r m t -> p r t m"
+                        ),
+                        g_raw[c][:, :, lo : lo + r_count // 2, j, :].rearrange("p t r m -> p r t m"),
+                    )
+                    for lo in (0, r_count // 2)
+                ]
+                quantise = dict(
                     out=g_codes[:, j, r_range, :].rearrange("p r m -> p (r m)").bitcast(E5M2_X4),
                     scales=g_scales[:, j, r_range, :].rearrange("p r m -> p (r m)"),
                     in_=g_grouped[:, j, r_range, :, :].rearrange("p r m t -> p (r m t)"),
                 )
+                pieces.append((copies, quantise))
+
+        waiting = None
+        for copies, quantise in pieces:
+            nc.vector.tensor_copy(out=copies[0][0], in_=copies[0][1])
+            nc.scalar.copy(out=copies[1][0], in_=copies[1][1])
+            if waiting is not None:
+                nc.vector.quantize_mx(**waiting)
+            waiting = quantise
+        nc.vector.quantize_mx(**waiting)
 
         for j in range(BLOCKS):
             acc = psum.tile([P, R, M], F32)

@@ -22,8 +22,8 @@ R = 64
 M = 8
 L1 = R * M
 
-R_CHUNKS = (16, 16, 32)
-assert sum(R_CHUNKS) == R
+G_CHUNKS = 2
+R_CHUNK = R // G_CHUNKS
 
 FLOPS = 2 * BLOCKS * K1 * L1 * SAMPLES
 BYTES = 2 * SAMPLES * BLOCKS * K1 + 2 * SAMPLES * BLOCKS * L1 + 4 * BLOCKS * K1 * L1
@@ -40,13 +40,11 @@ def tile_switchnet_fstar_pa_s_kernel(tc, x, k1, b1, grad_out, out):
         )
         g_rows = grad_out.rearrange("(p t) a c -> p t (a c)", t=PACK)
         g_raw = []
-        r_first = []
-        for c, r_count in enumerate(R_CHUNKS):
-            r_first.append(sum(R_CHUNKS[:c]))
-            chunk = keep.tile([P, PACK, r_count, BLOCKS, M], BF16, name="g_raw%d" % c)
+        for c in range(G_CHUNKS):
+            chunk = keep.tile([P, PACK, R_CHUNK, BLOCKS, M], BF16, name="g_raw%d" % c)
             nc.sync.dma_start(
                 out=chunk[:].rearrange("p t r j m -> p t (r j m)"),
-                in_=g_rows[:, :, r_first[c] * BLOCKS * M : (r_first[c] + r_count) * BLOCKS * M],
+                in_=g_rows[:, :, c * R_CHUNK * BLOCKS * M : (c + 1) * R_CHUNK * BLOCKS * M],
             )
             g_raw.append(chunk)
 
@@ -72,17 +70,17 @@ def tile_switchnet_fstar_pa_s_kernel(tc, x, k1, b1, grad_out, out):
                 in_=x_grouped[:, j].rearrange("p w h i t -> p (w h i t)"),
             )
             pieces.append((copies, quantise))
-        for c, r_count in enumerate(R_CHUNKS):
-            r_range = slice(r_first[c], r_first[c] + r_count)
+        for c in range(G_CHUNKS):
+            r_range = slice(c * R_CHUNK, (c + 1) * R_CHUNK)
             for j in range(BLOCKS):
                 copies = [
                     (
-                        g_grouped[:, j, r_first[c] + lo : r_first[c] + lo + r_count // 2, :, :].rearrange(
+                        g_grouped[:, j, c * R_CHUNK + lo : c * R_CHUNK + lo + R_CHUNK // 2, :, :].rearrange(
                             "p r m t -> p r t m"
                         ),
-                        g_raw[c][:, :, lo : lo + r_count // 2, j, :].rearrange("p t r m -> p r t m"),
+                        g_raw[c][:, :, lo : lo + R_CHUNK // 2, j, :].rearrange("p t r m -> p r t m"),
                     )
-                    for lo in (0, r_count // 2)
+                    for lo in (0, R_CHUNK // 2)
                 ]
                 quantise = dict(
                     out=g_codes[:, j, r_range, :].rearrange("p r m -> p (r m)").bitcast(E5M2_X4),

@@ -11,101 +11,104 @@ P = 128
 PACK = 4
 SAMPLES = P * PACK
 
-BLOCKS = 4
-BLOCK_SIDE = 2
+WINDOWS = 4
+GRID_WINDOWS = 2
 WINDOW_ROWS = 8
-HALVES = 2
 RUN = 8
-K1 = WINDOW_ROWS * HALVES * RUN
+ROW_RUNS = 2
+K1 = WINDOW_ROWS * ROW_RUNS * RUN
 
 R = 64
-M = 8
+M = RUN
 L1 = R * M
 
 G_CHUNKS = 2
 R_CHUNK = R // G_CHUNKS
+R_SHARE = R_CHUNK // 2
 
-FLOPS = 2 * BLOCKS * K1 * L1 * SAMPLES
-BYTES = 2 * SAMPLES * BLOCKS * K1 + 2 * SAMPLES * BLOCKS * L1 + 4 * BLOCKS * K1 * L1
+FLOPS = 2 * WINDOWS * K1 * L1 * SAMPLES
+BYTES = 2 * SAMPLES * WINDOWS * K1 + 2 * SAMPLES * WINDOWS * L1 + 4 * WINDOWS * K1 * L1
 
 
 def tile_switchnet_fstar_pa_s_kernel(tc, x, k1, b1, grad_out, out):
     nc = tc.nc
 
-    with tc.tile_pool(name="keep", bufs=1) as keep, tc.psum_pool(name="psum", bufs=BLOCKS) as psum, tc.manual_schedule():
-        x_raw = keep.tile([P, PACK, BLOCK_SIDE, WINDOW_ROWS, BLOCK_SIDE, HALVES, RUN], BF16)
+    keep_pool = tc.tile_pool(name="keep", bufs=1)
+    psum_pool = tc.psum_pool(name="psum", bufs=WINDOWS)
+    with keep_pool as keep, psum_pool as psum, tc.manual_schedule():
+        x_raw = keep.tile([P, PACK, GRID_WINDOWS, WINDOW_ROWS, GRID_WINDOWS, ROW_RUNS, RUN], BF16)
         nc.sync.dma_start(
-            out=x_raw[:].rearrange("p t a w b h i -> p t (a w b h i)"),
-            in_=x.rearrange("(p t) g c -> p t (g c)", t=PACK),
+            out=x_raw[:].rearrange("p t a w b u i -> p t (a w b u i)"),
+            in_=x.rearrange("(p t) g e -> p t (g e)", t=PACK),
         )
-        g_rows = grad_out.rearrange("(p t) a c -> p t (a c)", t=PACK)
+        g_rows = grad_out.rearrange("(p t) y z -> p t (y z)", t=PACK)
         g_raw = []
         for c in range(G_CHUNKS):
-            chunk = keep.tile([P, PACK, R_CHUNK, BLOCKS, M], BF16, name="g_raw%d" % c)
+            chunk = keep.tile([P, PACK, R_CHUNK, WINDOWS, M], BF16, name="g_raw%d" % c)
             nc.sync.dma_start(
                 out=chunk[:].rearrange("p t r j m -> p t (r j m)"),
-                in_=g_rows[:, :, c * R_CHUNK * BLOCKS * M : (c + 1) * R_CHUNK * BLOCKS * M],
+                in_=g_rows[:, :, c * R_CHUNK * WINDOWS * M : (c + 1) * R_CHUNK * WINDOWS * M],
             )
             g_raw.append(chunk)
 
-        x_grouped = keep.tile([P, BLOCKS, WINDOW_ROWS, HALVES, RUN, PACK], BF16, align_bytes=64)
-        x_codes = keep.tile([P, BLOCKS, K1], U32, align_bytes=64)
-        x_scales = keep.tile([P, BLOCKS, K1], U8, align_bytes=64)
-        g_grouped = keep.tile([P, BLOCKS, R, M, PACK], BF16, align_bytes=64)
-        g_codes = keep.tile([P, BLOCKS, R, M], U32, align_bytes=64)
-        g_scales = keep.tile([P, BLOCKS, R, M], U8, align_bytes=64)
+        h_grouped = keep.tile([P, WINDOWS, WINDOW_ROWS, ROW_RUNS, RUN, PACK], BF16, align_bytes=64)
+        h_codes = keep.tile([P, WINDOWS, K1], U32, align_bytes=64)
+        h_scales = keep.tile([P, WINDOWS, K1], U8, align_bytes=64)
+        gy_grouped = keep.tile([P, WINDOWS, R, M, PACK], BF16, align_bytes=64)
+        gy_codes = keep.tile([P, WINDOWS, R, M], U32, align_bytes=64)
+        gy_scales = keep.tile([P, WINDOWS, R, M], U8, align_bytes=64)
 
         pieces = []
-        for j in range(BLOCKS):
-            copies = [
-                (
-                    x_grouped[:, j, :, h, :, :].rearrange("p w i t -> p w t i"),
-                    x_raw[:, :, j // BLOCK_SIDE, :, j % BLOCK_SIDE, h, :].rearrange("p t w i -> p w t i"),
+        for j in range(WINDOWS):
+            vector_copy, scalar_copy = [
+                dict(
+                    out=h_grouped[:, j, :, u, :, :].rearrange("p w i t -> p w t i"),
+                    in_=x_raw[:, :, j // GRID_WINDOWS, :, j % GRID_WINDOWS, u, :].rearrange("p t w i -> p w t i"),
                 )
-                for h in range(HALVES)
+                for u in range(ROW_RUNS)
             ]
             quantise = dict(
-                out=x_codes[:, j, :].bitcast(E4M3_X4),
-                scales=x_scales[:, j, :],
-                in_=x_grouped[:, j].rearrange("p w h i t -> p (w h i t)"),
+                out=h_codes[:, j, :].bitcast(E4M3_X4),
+                scales=h_scales[:, j, :],
+                in_=h_grouped[:, j].rearrange("p w u i t -> p (w u i t)"),
             )
-            pieces.append((copies, quantise))
+            pieces.append((vector_copy, scalar_copy, quantise))
         for c in range(G_CHUNKS):
             r_range = slice(c * R_CHUNK, (c + 1) * R_CHUNK)
-            for j in range(BLOCKS):
-                copies = [
-                    (
-                        g_grouped[:, j, c * R_CHUNK + lo : c * R_CHUNK + lo + R_CHUNK // 2, :, :].rearrange(
+            for j in range(WINDOWS):
+                vector_copy, scalar_copy = [
+                    dict(
+                        out=gy_grouped[:, j, c * R_CHUNK + first : c * R_CHUNK + first + R_SHARE, :, :].rearrange(
                             "p r m t -> p r t m"
                         ),
-                        g_raw[c][:, :, lo : lo + R_CHUNK // 2, j, :].rearrange("p t r m -> p r t m"),
+                        in_=g_raw[c][:, :, first : first + R_SHARE, j, :].rearrange("p t r m -> p r t m"),
                     )
-                    for lo in (0, R_CHUNK // 2)
+                    for first in (0, R_SHARE)
                 ]
                 quantise = dict(
-                    out=g_codes[:, j, r_range, :].rearrange("p r m -> p (r m)").bitcast(E5M2_X4),
-                    scales=g_scales[:, j, r_range, :].rearrange("p r m -> p (r m)"),
-                    in_=g_grouped[:, j, r_range, :, :].rearrange("p r m t -> p (r m t)"),
+                    out=gy_codes[:, j, r_range, :].rearrange("p r m -> p (r m)").bitcast(E5M2_X4),
+                    scales=gy_scales[:, j, r_range, :].rearrange("p r m -> p (r m)"),
+                    in_=gy_grouped[:, j, r_range, :, :].rearrange("p r m t -> p (r m t)"),
                 )
-                pieces.append((copies, quantise))
+                pieces.append((vector_copy, scalar_copy, quantise))
 
         waiting = None
-        for copies, quantise in pieces:
-            nc.vector.tensor_copy(out=copies[0][0], in_=copies[0][1])
-            nc.scalar.copy(out=copies[1][0], in_=copies[1][1])
+        for vector_copy, scalar_copy, quantise in pieces:
+            nc.vector.tensor_copy(**vector_copy)
+            nc.scalar.copy(**scalar_copy)
             if waiting is not None:
                 nc.vector.quantize_mx(**waiting)
             waiting = quantise
         nc.vector.quantize_mx(**waiting)
 
-        for j in range(BLOCKS):
+        for j in range(WINDOWS):
             acc = psum.tile([P, R, M], F32)
             nc.tensor.matmul_mx(
                 out=acc[:].rearrange("p r m -> p (r m)"),
-                lhsT=x_codes[:, j, :].bitcast(E4M3_X4),
-                lhsT_scale=x_scales[:, j, :],
-                rhs=g_codes[:, j, :, :].rearrange("p r m -> p (r m)").bitcast(E5M2_X4),
-                rhs_scale=g_scales[:, j, :, :].rearrange("p r m -> p (r m)"),
+                lhsT=h_codes[:, j, :].bitcast(E4M3_X4),
+                lhsT_scale=h_scales[:, j, :],
+                rhs=gy_codes[:, j, :, :].rearrange("p r m -> p (r m)").bitcast(E5M2_X4),
+                rhs_scale=gy_scales[:, j, :, :].rearrange("p r m -> p (r m)"),
                 start=True,
                 stop=True,
             )

@@ -26,6 +26,9 @@ G_CHUNKS = 2
 R_CHUNK = R // G_CHUNKS
 R_SHARE = R_CHUNK // 2
 
+WARM_COLUMNS = 128
+WARM_PIECES = (4, 5, 6, 7, 8)
+
 FLOPS = 2 * WINDOWS * K1 * L1 * SAMPLES
 BYTES = 2 * SAMPLES * WINDOWS * K1 + 2 * SAMPLES * WINDOWS * L1 + 4 * WINDOWS * K1 * L1
 
@@ -35,7 +38,8 @@ def tile_switchnet_fstar_pa_s_kernel(tc, x, k1, b1, grad_out, out):
 
     keep_pool = tc.tile_pool(name="keep", bufs=1)
     psum_pool = tc.psum_pool(name="psum", bufs=WINDOWS)
-    with keep_pool as keep, psum_pool as psum, tc.manual_schedule():
+    warm_pool = tc.psum_pool(name="warm", bufs=1)
+    with keep_pool as keep, psum_pool as psum, warm_pool as warm_psum, tc.manual_schedule():
         x_raw = keep.tile([P, PACK, GRID_WINDOWS, WINDOW_ROWS, GRID_WINDOWS, ROW_RUNS, RUN], BF16)
         nc.sync.dma_start(
             out=x_raw[:].rearrange("p t a w b u i -> p t (a w b u i)"),
@@ -92,13 +96,22 @@ def tile_switchnet_fstar_pa_s_kernel(tc, x, k1, b1, grad_out, out):
                 )
                 pieces.append((vector_copy, scalar_copy, quantise))
 
+        zeros = keep.tile([P, P], F32)
+        nc.vector.memset(zeros[:], 0.0)
+        idle_sums = warm_psum.tile([P, WARM_COLUMNS], F32)
         waiting = None
-        for vector_copy, scalar_copy, quantise in pieces:
+        for number, (vector_copy, scalar_copy, quantise) in enumerate(pieces):
             nc.vector.tensor_copy(**vector_copy)
             nc.scalar.copy(**scalar_copy)
             if waiting is not None:
                 nc.vector.quantize_mx(**waiting)
             waiting = quantise
+            if number in WARM_PIECES:
+                c, j = (number - WINDOWS) // WINDOWS, (number - WINDOWS) % WINDOWS
+                fresh = gy_grouped[:, j, c * R_CHUNK : c * R_CHUNK + R_SHARE, :, :].rearrange("p r m t -> p (r m t)")
+                nc.tensor.matmul(
+                    out=idle_sums[:], lhsT=zeros[:], rhs=fresh.bitcast(F32)[:, 0:WARM_COLUMNS], start=True, stop=True
+                )
         nc.vector.quantize_mx(**waiting)
 
         for j in range(WINDOWS):

@@ -27,7 +27,6 @@ R_CHUNK = R // G_CHUNKS
 R_SHARE = R_CHUNK // 2
 
 WARM_COLUMNS = 128
-WARM_PIECES = (4, 5, 6, 7, 8)
 
 FLOPS = 2 * WINDOWS * K1 * L1 * SAMPLES
 BYTES = 2 * SAMPLES * WINDOWS * K1 + 2 * SAMPLES * WINDOWS * L1 + 4 * WINDOWS * K1 * L1
@@ -62,59 +61,46 @@ def tile_switchnet_fstar_pa_s_kernel(tc, x, k1, b1, grad_out, out):
         gy_codes = keep.tile([P, WINDOWS, R, M], U32, align_bytes=64)
         gy_scales = keep.tile([P, WINDOWS, R, M], U8, align_bytes=64)
 
-        pieces = []
-        for j in range(WINDOWS):
-            vector_copy, scalar_copy = [
-                dict(
-                    out=h_grouped[:, j, :, u, :, :].rearrange("p w i t -> p w t i"),
-                    in_=x_raw[:, :, j // GRID_WINDOWS, :, j % GRID_WINDOWS, u, :].rearrange("p t w i -> p w t i"),
-                )
-                for u in range(ROW_RUNS)
-            ]
-            quantise = dict(
+        def h_copy(j, u):
+            return dict(
+                out=h_grouped[:, j, :, u, :, :].rearrange("p w i t -> p w t i"),
+                in_=x_raw[:, :, j // GRID_WINDOWS, :, j % GRID_WINDOWS, u, :].rearrange("p t w i -> p w t i"),
+            )
+
+        def h_quantise(j):
+            return dict(
                 out=h_codes[:, j, :].bitcast(E4M3_X4),
                 scales=h_scales[:, j, :],
                 in_=h_grouped[:, j].rearrange("p w u i t -> p (w u i t)"),
             )
-            pieces.append((vector_copy, scalar_copy, quantise))
-        for c in range(G_CHUNKS):
+
+        def g_copy(c, j, r0, r1):
+            return dict(
+                out=gy_grouped[:, j, c * R_CHUNK + r0 : c * R_CHUNK + r1, :, :].rearrange("p r m t -> p r t m"),
+                in_=g_raw[c][:, :, r0:r1, j, :].rearrange("p t r m -> p r t m"),
+            )
+
+        def g_quantise(c, j):
             r_range = slice(c * R_CHUNK, (c + 1) * R_CHUNK)
-            for j in range(WINDOWS):
-                vector_copy, scalar_copy = [
-                    dict(
-                        out=gy_grouped[:, j, c * R_CHUNK + first : c * R_CHUNK + first + R_SHARE, :, :].rearrange(
-                            "p r m t -> p r t m"
-                        ),
-                        in_=g_raw[c][:, :, first : first + R_SHARE, j, :].rearrange("p t r m -> p r t m"),
-                    )
-                    for first in (0, R_SHARE)
-                ]
-                quantise = dict(
-                    out=gy_codes[:, j, r_range, :].rearrange("p r m -> p (r m)").bitcast(E5M2_X4),
-                    scales=gy_scales[:, j, r_range, :].rearrange("p r m -> p (r m)"),
-                    in_=gy_grouped[:, j, r_range, :, :].rearrange("p r m t -> p (r m t)"),
-                )
-                pieces.append((vector_copy, scalar_copy, quantise))
+            return dict(
+                out=gy_codes[:, j, r_range, :].rearrange("p r m -> p (r m)").bitcast(E5M2_X4),
+                scales=gy_scales[:, j, r_range, :].rearrange("p r m -> p (r m)"),
+                in_=gy_grouped[:, j, r_range, :, :].rearrange("p r m t -> p (r m t)"),
+            )
 
         zeros = keep.tile([P, P], F32)
         nc.vector.memset(zeros[:], 0.0)
         idle_sums = warm_psum.tile([P, WARM_COLUMNS], F32)
-        waiting = None
-        for number, (vector_copy, scalar_copy, quantise) in enumerate(pieces):
-            nc.vector.tensor_copy(**vector_copy)
-            nc.scalar.copy(**scalar_copy)
-            if waiting is not None:
-                nc.vector.quantize_mx(**waiting)
-            waiting = quantise
-            if number in WARM_PIECES:
-                c, j = (number - WINDOWS) // WINDOWS, (number - WINDOWS) % WINDOWS
-                fresh = gy_grouped[:, j, c * R_CHUNK : c * R_CHUNK + R_SHARE, :, :].rearrange("p r m t -> p (r m t)")
-                nc.tensor.matmul(
-                    out=idle_sums[:], lhsT=zeros[:], rhs=fresh.bitcast(F32)[:, 0:WARM_COLUMNS], start=True, stop=True
-                )
-        nc.vector.quantize_mx(**waiting)
 
-        for j in range(WINDOWS):
+        def warm(c, j):
+            fresh = gy_grouped[:, j, c * R_CHUNK : c * R_CHUNK + R_SHARE, :, :].rearrange("p r m t -> p (r m t)")
+            nc.tensor.matmul(
+                out=idle_sums[:], lhsT=zeros[:], rhs=fresh.bitcast(F32)[:, 0:WARM_COLUMNS], start=True, stop=True
+            )
+
+        accs = []
+
+        def multiply(j):
             acc = psum.tile([P, R, M], F32)
             nc.tensor.matmul_mx(
                 out=acc[:].rearrange("p r m -> p (r m)"),
@@ -125,9 +111,42 @@ def tile_switchnet_fstar_pa_s_kernel(tc, x, k1, b1, grad_out, out):
                 start=True,
                 stop=True,
             )
+            accs.append(acc)
+
+        def leave(j, engine_copy):
             result = keep.tile([P, M, R], F32, name="result%d" % j)
-            if j % 2 == 0:
-                nc.scalar.copy(out=result[:], in_=acc[:].rearrange("p r m -> p m r"))
-            else:
-                nc.vector.tensor_copy(out=result[:], in_=acc[:].rearrange("p r m -> p m r"))
+            engine_copy(out=result[:], in_=accs[j][:].rearrange("p r m -> p m r"))
             nc.sync.dma_start(out=out[j], in_=result[:].rearrange("p m r -> p (m r)"))
+
+        vcopy = nc.vector.tensor_copy
+        scopy = nc.scalar.copy
+        quant = nc.vector.quantize_mx
+
+        for j in range(WINDOWS):
+            vcopy(**h_copy(j, 0))
+            scopy(**h_copy(j, 1))
+            if j > 0:
+                quant(**h_quantise(j - 1))
+        for j in range(WINDOWS):
+            vcopy(**g_copy(0, j, 0, R_SHARE))
+            scopy(**g_copy(0, j, R_SHARE, R_CHUNK))
+            quant(**(g_quantise(0, j - 1) if j > 0 else h_quantise(WINDOWS - 1)))
+            warm(0, j)
+        for j in range(WINDOWS - 1):
+            vcopy(**g_copy(1, j, 0, R_SHARE))
+            scopy(**g_copy(1, j, R_SHARE, R_CHUNK))
+            if j == 0:
+                quant(**g_quantise(0, WINDOWS - 1))
+                warm(1, 0)
+            else:
+                quant(**g_quantise(1, j - 1))
+                multiply(j - 1)
+        vcopy(**g_copy(1, WINDOWS - 1, 0, R_CHUNK))
+        quant(**g_quantise(1, WINDOWS - 2))
+        multiply(WINDOWS - 2)
+        leave(0, scopy)
+        leave(1, scopy)
+        quant(**g_quantise(1, WINDOWS - 1))
+        multiply(WINDOWS - 1)
+        leave(2, scopy)
+        leave(3, vcopy)

@@ -25,6 +25,7 @@ L1 = R * M
 G_CHUNKS = 2
 R_CHUNK = R // G_CHUNKS
 R_SHARE = R_CHUNK // 2
+LAST_SHARE = 24
 
 WARM_COLUMNS = 128
 
@@ -127,25 +128,25 @@ def tile_switchnet_fstar_pa_s_kernel(tc, x, k1, b1, grad_out, out):
             scopy(**h_copy(j, 1))
             if j > 0:
                 quant(**h_quantise(j - 1))
+        quant(**h_quantise(WINDOWS - 1))
         for j in range(WINDOWS):
             vcopy(**g_copy(0, j, 0, R_SHARE))
             scopy(**g_copy(0, j, R_SHARE, R_CHUNK))
-            quant(**(g_quantise(0, j - 1) if j > 0 else h_quantise(WINDOWS - 1)))
             warm(0, j)
         for j in range(WINDOWS - 1):
-            vcopy(**g_copy(1, j, 0, R_SHARE))
-            scopy(**g_copy(1, j, R_SHARE, R_CHUNK))
+            quant(**g_quantise(0, j))
+        for j in range(WINDOWS):
+            share = R_SHARE if j < WINDOWS - 1 else LAST_SHARE
+            vcopy(**g_copy(1, j, 0, share))
+            scopy(**g_copy(1, j, share, R_CHUNK))
             if j == 0:
-                quant(**g_quantise(0, WINDOWS - 1))
                 warm(1, 0)
             else:
                 quant(**g_quantise(1, j - 1))
                 multiply(j - 1)
-        vcopy(**g_copy(1, WINDOWS - 1, 0, R_CHUNK))
-        quant(**g_quantise(1, WINDOWS - 2))
-        multiply(WINDOWS - 2)
         leave(0, scopy)
         leave(1, scopy)
+        quant(**g_quantise(0, WINDOWS - 1))
         quant(**g_quantise(1, WINDOWS - 1))
         multiply(WINDOWS - 1)
         leave(2, scopy)

@@ -24,8 +24,7 @@ L1 = R * M
 
 G_CHUNKS = 2
 R_CHUNK = R // G_CHUNKS
-R_SHARE = R_CHUNK // 2
-LAST_SHARE = 24
+R_SHARES = ((18, 18, 18, 18), (20, 20, 8, 32))
 
 WARM_COLUMNS = 128
 
@@ -94,7 +93,7 @@ def tile_switchnet_fstar_pa_s_kernel(tc, x, k1, b1, grad_out, out):
         idle_sums = warm_psum.tile([P, WARM_COLUMNS], F32)
 
         def warm(c, j):
-            fresh = gy_grouped[:, j, c * R_CHUNK : c * R_CHUNK + R_SHARE, :, :].rearrange("p r m t -> p (r m t)")
+            fresh = gy_grouped[:, j, c * R_CHUNK : c * R_CHUNK + 8, :, :].rearrange("p r m t -> p (r m t)")
             nc.tensor.matmul(
                 out=idle_sums[:], lhsT=zeros[:], rhs=fresh.bitcast(F32)[:, 0:WARM_COLUMNS], start=True, stop=True
             )
@@ -130,15 +129,16 @@ def tile_switchnet_fstar_pa_s_kernel(tc, x, k1, b1, grad_out, out):
                 quant(**h_quantise(j - 1))
         quant(**h_quantise(WINDOWS - 1))
         for j in range(WINDOWS):
-            vcopy(**g_copy(0, j, 0, R_SHARE))
-            scopy(**g_copy(0, j, R_SHARE, R_CHUNK))
+            vcopy(**g_copy(0, j, 0, R_SHARES[0][j]))
+            scopy(**g_copy(0, j, R_SHARES[0][j], R_CHUNK))
             warm(0, j)
         for j in range(WINDOWS - 1):
             quant(**g_quantise(0, j))
         for j in range(WINDOWS):
-            share = R_SHARE if j < WINDOWS - 1 else LAST_SHARE
+            share = R_SHARES[1][j]
             vcopy(**g_copy(1, j, 0, share))
-            scopy(**g_copy(1, j, share, R_CHUNK))
+            if share < R_CHUNK:
+                scopy(**g_copy(1, j, share, R_CHUNK))
             if j == 0:
                 warm(1, 0)
             else:

@@ -26,6 +26,7 @@ G_CHUNKS = 2
 R_CHUNK = R // G_CHUNKS
 R_SHARES = ((18, 18, 18, 18), (20, 20, 8, 32))
 
+M_VECTOR = 4
 WARM_COLUMNS = 128
 
 FLOPS = 2 * WINDOWS * K1 * L1 * SAMPLES
@@ -36,7 +37,7 @@ def tile_switchnet_fstar_pa_s_kernel(tc, x, k1, b1, grad_out, out):
     nc = tc.nc
 
     keep_pool = tc.tile_pool(name="keep", bufs=1)
-    psum_pool = tc.psum_pool(name="psum", bufs=WINDOWS)
+    psum_pool = tc.psum_pool(name="psum", bufs=WINDOWS + 1)
     warm_pool = tc.psum_pool(name="warm", bufs=1)
     with keep_pool as keep, psum_pool as psum, warm_pool as warm_psum, tc.manual_schedule():
         x_raw = keep.tile([P, PACK, GRID_WINDOWS, WINDOW_ROWS, GRID_WINDOWS, ROW_RUNS, RUN], BF16)
@@ -118,6 +119,11 @@ def tile_switchnet_fstar_pa_s_kernel(tc, x, k1, b1, grad_out, out):
             engine_copy(out=result[:], in_=accs[j][:].rearrange("p r m -> p m r"))
             nc.sync.dma_start(out=out[j], in_=result[:].rearrange("p m r -> p (m r)"))
 
+        def leave_part(bank, m0, m1, engine_copy):
+            part = keep.tile([P, m1 - m0, R], F32, name="part%d" % bank)
+            engine_copy(out=part[:], in_=accs[bank][:, :, m0:m1].rearrange("p r m -> p m r"))
+            nc.sync.dma_start(out=out[WINDOWS - 1, :, m0 * R : m1 * R], in_=part[:].rearrange("p m r -> p (m r)"))
+
         vcopy = nc.vector.tensor_copy
         scopy = nc.scalar.copy
         quant = nc.vector.quantize_mx
@@ -149,5 +155,7 @@ def tile_switchnet_fstar_pa_s_kernel(tc, x, k1, b1, grad_out, out):
         quant(**g_quantise(0, WINDOWS - 1))
         quant(**g_quantise(1, WINDOWS - 1))
         multiply(WINDOWS - 1)
-        leave(2, scopy)
-        leave(3, vcopy)
+        multiply(WINDOWS - 1)
+        leave(2, vcopy)
+        leave_part(3, 0, M_VECTOR, vcopy)
+        leave_part(4, M_VECTOR, M, scopy)

import concourse.mybir as mybir

BF16 = mybir.dt.bfloat16
F32 = mybir.dt.float32
U32 = mybir.dt.uint32
U8 = mybir.dt.uint8
E4M3_X4 = mybir.dt.float8_e4m3fn_x4
E5M2_X4 = mybir.dt.float8_e5m2_x4

P = 128
PACK = 4
SAMPLES = P * PACK

WINDOWS = 4
GRID_WINDOWS = 2
WINDOW_ROWS = 8
RUN = 8
ROW_RUNS = 2
K1 = WINDOW_ROWS * ROW_RUNS * RUN

R = 64
M = RUN
L1 = R * M

G_CHUNKS = 2
R_CHUNK = R // G_CHUNKS
R_SHARES = ((18, 18, 18, 18), (20, 20, 8, 32))

M_VECTOR = 4
WARM_COLUMNS = 128

FLOPS = 2 * WINDOWS * K1 * L1 * SAMPLES
BYTES = 2 * SAMPLES * WINDOWS * K1 + 2 * SAMPLES * WINDOWS * L1 + 4 * WINDOWS * K1 * L1


def tile_switchnet_fstar_pa_s_kernel(tc, x, k1, b1, grad_out, out):
    nc = tc.nc

    keep_pool = tc.tile_pool(name="keep", bufs=1)
    psum_pool = tc.psum_pool(name="psum", bufs=WINDOWS + 1)
    warm_pool = tc.psum_pool(name="warm", bufs=1)
    with keep_pool as keep, psum_pool as psum, warm_pool as warm_psum, tc.manual_schedule():
        x_raw = keep.tile([P, PACK, GRID_WINDOWS, WINDOW_ROWS, GRID_WINDOWS, ROW_RUNS, RUN], BF16)
        nc.sync.dma_start(
            out=x_raw[:].rearrange("p t a w b u i -> p t (a w b u i)"),
            in_=x.rearrange("(p t) g e -> p t (g e)", t=PACK),
        )
        g_rows = grad_out.rearrange("(p t) y z -> p t (y z)", t=PACK)
        g_raw = []
        for c in range(G_CHUNKS):
            chunk = keep.tile([P, PACK, R_CHUNK, WINDOWS, M], BF16, name="g_raw%d" % c)
            nc.sync.dma_start(
                out=chunk[:].rearrange("p t r j m -> p t (r j m)"),
                in_=g_rows[:, :, c * R_CHUNK * WINDOWS * M : (c + 1) * R_CHUNK * WINDOWS * M],
            )
            g_raw.append(chunk)

        h_grouped = keep.tile([P, WINDOWS, WINDOW_ROWS, ROW_RUNS, RUN, PACK], BF16, align_bytes=64)
        h_codes = keep.tile([P, WINDOWS, K1], U32, align_bytes=64)
        h_scales = keep.tile([P, WINDOWS, K1], U8, align_bytes=64)
        gy_grouped = keep.tile([P, WINDOWS, R, M, PACK], BF16, align_bytes=64)
        gy_codes = keep.tile([P, WINDOWS, R, M], U32, align_bytes=64)
        gy_scales = keep.tile([P, WINDOWS, R, M], U8, align_bytes=64)

        def h_copy(j, u):
            return dict(
                out=h_grouped[:, j, :, u, :, :].rearrange("p w i t -> p w t i"),
                in_=x_raw[:, :, j // GRID_WINDOWS, :, j % GRID_WINDOWS, u, :].rearrange("p t w i -> p w t i"),
            )

        def h_quantise(j):
            return dict(
                out=h_codes[:, j, :].bitcast(E4M3_X4),
                scales=h_scales[:, j, :],
                in_=h_grouped[:, j].rearrange("p w u i t -> p (w u i t)"),
            )

        def g_copy(c, j, r0, r1):
            return dict(
                out=gy_grouped[:, j, c * R_CHUNK + r0 : c * R_CHUNK + r1, :, :].rearrange("p r m t -> p r t m"),
                in_=g_raw[c][:, :, r0:r1, j, :].rearrange("p t r m -> p r t m"),
            )

        def g_quantise(c, j):
            r_range = slice(c * R_CHUNK, (c + 1) * R_CHUNK)
            return dict(
                out=gy_codes[:, j, r_range, :].rearrange("p r m -> p (r m)").bitcast(E5M2_X4),
                scales=gy_scales[:, j, r_range, :].rearrange("p r m -> p (r m)"),
                in_=gy_grouped[:, j, r_range, :, :].rearrange("p r m t -> p (r m t)"),
            )

        zeros = keep.tile([P, P], F32)
        nc.vector.memset(zeros[:], 0.0)
        idle_sums = warm_psum.tile([P, WARM_COLUMNS], F32)

        def warm(c, j):
            fresh = gy_grouped[:, j, c * R_CHUNK : c * R_CHUNK + 8, :, :].rearrange("p r m t -> p (r m t)")
            nc.tensor.matmul(
                out=idle_sums[:], lhsT=zeros[:], rhs=fresh.bitcast(F32)[:, 0:WARM_COLUMNS], start=True, stop=True
            )

        accs = []

        def multiply(j):
            acc = psum.tile([P, R, M], F32)
            nc.tensor.matmul_mx(
                out=acc[:].rearrange("p r m -> p (r m)"),
                lhsT=h_codes[:, j, :].bitcast(E4M3_X4),
                lhsT_scale=h_scales[:, j, :],
                rhs=gy_codes[:, j, :, :].rearrange("p r m -> p (r m)").bitcast(E5M2_X4),
                rhs_scale=gy_scales[:, j, :, :].rearrange("p r m -> p (r m)"),
                start=True,
                stop=True,
            )
            accs.append(acc)

        def leave(j, engine_copy):
            result = keep.tile([P, M, R], F32, name="result%d" % j)
            engine_copy(out=result[:], in_=accs[j][:].rearrange("p r m -> p m r"))
            nc.sync.dma_start(out=out[j], in_=result[:].rearrange("p m r -> p (m r)"))

        def leave_part(bank, m0, m1, engine_copy):
            part = keep.tile([P, m1 - m0, R], F32, name="part%d" % bank)
            engine_copy(out=part[:], in_=accs[bank][:, :, m0:m1].rearrange("p r m -> p m r"))
            nc.sync.dma_start(out=out[WINDOWS - 1, :, m0 * R : m1 * R], in_=part[:].rearrange("p m r -> p (m r)"))

        vcopy = nc.vector.tensor_copy
        scopy = nc.scalar.copy
        quant = nc.vector.quantize_mx

        for j in range(WINDOWS):
            vcopy(**h_copy(j, 0))
            scopy(**h_copy(j, 1))
            if j > 0:
                quant(**h_quantise(j - 1))
        quant(**h_quantise(WINDOWS - 1))
        for j in range(WINDOWS):
            vcopy(**g_copy(0, j, 0, R_SHARES[0][j]))
            scopy(**g_copy(0, j, R_SHARES[0][j], R_CHUNK))
            warm(0, j)
        for j in range(WINDOWS - 1):
            quant(**g_quantise(0, j))
        for j in range(WINDOWS):
            share = R_SHARES[1][j]
            vcopy(**g_copy(1, j, 0, share))
            if share < R_CHUNK:
                scopy(**g_copy(1, j, share, R_CHUNK))
            if j == 0:
                warm(1, 0)
            else:
                quant(**g_quantise(1, j - 1))
                multiply(j - 1)
        leave(0, scopy)
        leave(1, scopy)
        quant(**g_quantise(0, WINDOWS - 1))
        quant(**g_quantise(1, WINDOWS - 1))
        multiply(WINDOWS - 1)
        multiply(WINDOWS - 1)
        leave(2, vcopy)
        leave_part(3, 0, M_VECTOR, vcopy)
        leave_part(4, M_VECTOR, M, scopy)
